import numpy as np
import ml_dtypes

BF16 = ml_dtypes.bfloat16


def bf(x):
    return np.asarray(x, np.float32).astype(BF16)


def f32(x):
    return np.asarray(x, np.float32)


def f64(x):
    return np.asarray(x).astype(np.float64)


def striped(idx):
    return np.tile(idx.reshape(-1, 16).T, (8, 1))


S, D, T, N = 256, 128, 128, 128


def setup_inputs():
    h = np.random.standard_normal(D // 2)
    h = h / np.sqrt(np.mean(h * h))
    vals = np.concatenate([h, -h])
    xn = np.stack([np.random.permutation(vals) for _ in range(T)], axis=1)
    return {"table": bf(np.random.standard_normal((S, D))), "xn": bf(xn), "key_w": bf(np.random.standard_normal((D, D)) / np.sqrt(D)), "key_b": f32(0.1 * np.random.standard_normal((D, 1))), "offs": striped(np.random.permutation(S)[:N])}


def reference(table, xn, key_w, key_b, offs):
    idx = offs[:16].T.reshape(-1)
    xk = f64(key_w).T @ f64(xn) + f64(key_b)
    picked = xk.T @ f64(table)[idx].T
    cross = xk.T @ f64(xn)
    return ((picked[:, None, :] + cross[:, :, None]) / np.sqrt(D)).reshape(T, T * N)

@@ -1,0 +1,63 @@
+import math
+
+import concourse.mybir as mybir
+from concourse.masks import make_identity
+
+S, D, T, N = 256, 128, 128, 128
+P = 128
+BF16, F32, U16 = mybir.dt.bfloat16, mybir.dt.float32, mybir.dt.uint16
+IDENTITY = mybir.ActivationFunctionType.Identity
+INV_SQRT_D = 1.0 / math.sqrt(D)
+POSITIONS_PER_STORE = 8
+
+FLOPS = 2 * D * D * T + 2 * D * T * N + 2 * D * T * T
+
+
+def tile_end_expansionnet_v2_onnx_tensorrt_kernel(tc, table, xn, key_w, key_b, offs, out):
+    nc = tc.nc
+    stores = T // POSITIONS_PER_STORE
+    with (
+        tc.tile_pool(name="held", bufs=1) as held,
+        tc.tile_pool(name="stage", bufs=stores) as stage,
+        tc.psum_pool(name="psum", bufs=1) as psum,
+    ):
+        offsets = held.tile([P, N // 16], U16, name="offsets")
+        nc.sync.dma_start(offsets[:], offs)
+        xn_sb = held.tile([D, T], BF16, name="xn_sb")
+        nc.sync.dma_start(xn_sb[:], xn)
+        key_w_sb = held.tile([D, D], BF16, name="key_w_sb")
+        nc.scalar.dma_start(key_w_sb[:], key_w)
+        key_b_sb = held.tile([D, 1], F32, name="key_b_sb")
+        nc.scalar.dma_start(key_b_sb[:], key_b)
+        words = held.tile([P, S // P, D], BF16, name="words")
+        nc.gpsimd.dma_start(words[:], table.rearrange("(h p) d -> p h d", p=P))
+
+        identity = held.tile([P, P], BF16, name="identity")
+        make_identity(nc, identity[:])
+        table_t_ps = psum.tile([D, S], BF16, name="table_t_ps")
+        for h in range(S // P):
+            nc.tensor.transpose(table_t_ps[:, h * P : (h + 1) * P], words[:, h, :], identity[:])
+        table_t = held.tile([D, S], BF16, name="table_t")
+        nc.vector.tensor_copy(table_t[:], table_t_ps[:])
+
+        xk_ps = psum.tile([D, T], F32, name="xk_ps")
+        nc.tensor.matmul(xk_ps[:], key_w_sb[:], xn_sb[:], start=True, stop=True)
+        xk = held.tile([D, T], BF16, name="xk")
+        nc.scalar.activation(xk[:], xk_ps[:], IDENTITY, bias=key_b_sb[:, 0:1], scale=1.0)
+
+        p_ps = psum.tile([T, N], F32, name="p_ps")
+        nc.tensor.matmul(p_ps[:], xk[:], table_t[:].indirect(offsets[:]), start=True, stop=True)
+        q_ps = psum.tile([T, T], F32, name="q_ps")
+        nc.tensor.matmul(q_ps[:], xk[:], xn_sb[:], start=True, stop=True)
+
+        p_scaled = held.tile([T, N], F32, name="p_scaled")
+        nc.vector.tensor_scalar_mul(p_scaled[:], p_ps[:], INV_SQRT_D)
+        q_scaled = held.tile([T, T], F32, name="q_scaled")
+        nc.scalar.mul(q_scaled[:], q_ps[:], INV_SQRT_D)
+
+        for s in range(stores):
+            staged = stage.tile([P, POSITIONS_PER_STORE * N], F32, name="staged")
+            for k in range(POSITIONS_PER_STORE):
+                t = s * POSITIONS_PER_STORE + k
+                nc.vector.tensor_scalar_add(staged[:, k * N : (k + 1) * N], p_scaled[:], q_scaled[:, t : t + 1])
+            nc.sync.dma_start(out[:, s * POSITIONS_PER_STORE * N : (s + 1) * POSITIONS_PER_STORE * N], staged[:])

@@ -6,7 +6,6 @@ from concourse.masks import make_identity
 S, D, T, N = 256, 128, 128, 128
 P = 128
 BF16, F32, U16 = mybir.dt.bfloat16, mybir.dt.float32, mybir.dt.uint16
-IDENTITY = mybir.ActivationFunctionType.Identity
 INV_SQRT_D = 1.0 / math.sqrt(D)
 POSITIONS_PER_STORE = 8
 
@@ -21,39 +20,39 @@ def tile_end_expansionnet_v2_onnx_tensorrt_kernel(tc, table, xn, key_w, key_b, o
         tc.tile_pool(name="stage", bufs=stores) as stage,
         tc.psum_pool(name="psum", bufs=1) as psum,
     ):
+        words = held.tile([P, S // P, D], BF16, name="words")
+        nc.sync.dma_start(words[:], table.rearrange("(h p) d -> p h d", p=P))
         offsets = held.tile([P, N // 16], U16, name="offsets")
         nc.sync.dma_start(offsets[:], offs)
-        xn_sb = held.tile([D, T], BF16, name="xn_sb")
-        nc.sync.dma_start(xn_sb[:], xn)
-        key_w_sb = held.tile([D, D], BF16, name="key_w_sb")
-        nc.scalar.dma_start(key_w_sb[:], key_w)
         key_b_sb = held.tile([D, 1], F32, name="key_b_sb")
         nc.scalar.dma_start(key_b_sb[:], key_b)
-        words = held.tile([P, S // P, D], BF16, name="words")
-        nc.gpsimd.dma_start(words[:], table.rearrange("(h p) d -> p h d", p=P))
+        key_w_sb = held.tile([D, D], BF16, name="key_w_sb")
+        nc.scalar.dma_start(key_w_sb[:], key_w)
+        xn_sb = held.tile([D, T], BF16, name="xn_sb")
+        nc.scalar.dma_start(xn_sb[:], xn)
+
+        xk_ps = psum.tile([D, T], F32, name="xk_ps")
+        nc.tensor.matmul(xk_ps[:], key_w_sb[:], xn_sb[:], start=True, stop=True)
+        xk = held.tile([D, T], BF16, name="xk")
+        nc.vector.tensor_scalar_add(xk[:], xk_ps[:], key_b_sb[:, 0:1])
 
         identity = held.tile([P, P], BF16, name="identity")
-        make_identity(nc, identity[:])
+        nc.vector.memset(identity[:], 0.0)
+        make_identity(nc, identity[:], nomemset=True)
         table_t_ps = psum.tile([D, S], BF16, name="table_t_ps")
         for h in range(S // P):
             nc.tensor.transpose(table_t_ps[:, h * P : (h + 1) * P], words[:, h, :], identity[:])
         table_t = held.tile([D, S], BF16, name="table_t")
         nc.vector.tensor_copy(table_t[:], table_t_ps[:])
 
-        xk_ps = psum.tile([D, T], F32, name="xk_ps")
-        nc.tensor.matmul(xk_ps[:], key_w_sb[:], xn_sb[:], start=True, stop=True)
-        xk = held.tile([D, T], BF16, name="xk")
-        nc.scalar.activation(xk[:], xk_ps[:], IDENTITY, bias=key_b_sb[:, 0:1], scale=1.0)
-
-        p_ps = psum.tile([T, N], F32, name="p_ps")
-        nc.tensor.matmul(p_ps[:], xk[:], table_t[:].indirect(offsets[:]), start=True, stop=True)
         q_ps = psum.tile([T, T], F32, name="q_ps")
         nc.tensor.matmul(q_ps[:], xk[:], xn_sb[:], start=True, stop=True)
-
+        q_scaled = held.tile([T, T], F32, name="q_scaled")
+        nc.vector.tensor_scalar_mul(q_scaled[:], q_ps[:], INV_SQRT_D)
+        p_ps = psum.tile([T, N], F32, name="p_ps")
+        nc.tensor.matmul(p_ps[:], xk[:], table_t[:].indirect(offsets[:]), start=True, stop=True)
         p_scaled = held.tile([T, N], F32, name="p_scaled")
         nc.vector.tensor_scalar_mul(p_scaled[:], p_ps[:], INV_SQRT_D)
-        q_scaled = held.tile([T, T], F32, name="q_scaled")
-        nc.scalar.mul(q_scaled[:], q_ps[:], INV_SQRT_D)
 
         for s in range(stores):
             staged = stage.tile([P, POSITIONS_PER_STORE * N], F32, name="staged")

@@ -7,29 +7,38 @@ S, D, T, N = 256, 128, 128, 128
 P = 128
 BF16, F32, U16 = mybir.dt.bfloat16, mybir.dt.float32, mybir.dt.uint16
 INV_SQRT_D = 1.0 / math.sqrt(D)
-POSITIONS_PER_STORE = 8
+FIRST_PIECE = 4
+LARGEST_PIECE = 16
 
 FLOPS = 2 * D * D * T + 2 * D * T * N + 2 * D * T * T
 
 
+def store_pieces():
+    pieces = []
+    done = 0
+    while done < T:
+        count = min(max(done, FIRST_PIECE), LARGEST_PIECE, T - done)
+        pieces.append((done, count))
+        done += count
+    return pieces
+
+
 def tile_end_expansionnet_v2_onnx_tensorrt_kernel(tc, table, xn, key_w, key_b, offs, out):
     nc = tc.nc
-    stores = T // POSITIONS_PER_STORE
     with (
         tc.tile_pool(name="held", bufs=1) as held,
-        tc.tile_pool(name="stage", bufs=stores) as stage,
         tc.psum_pool(name="psum", bufs=1) as psum,
     ):
-        words = held.tile([P, S // P, D], BF16, name="words")
-        nc.sync.dma_start(words[:], table.rearrange("(h p) d -> p h d", p=P))
-        offsets = held.tile([P, N // 16], U16, name="offsets")
-        nc.sync.dma_start(offsets[:], offs)
-        key_b_sb = held.tile([D, 1], F32, name="key_b_sb")
-        nc.scalar.dma_start(key_b_sb[:], key_b)
+        xn_sb = held.tile([D, T], BF16, name="xn_sb")
+        nc.sync.dma_start(xn_sb[:], xn)
         key_w_sb = held.tile([D, D], BF16, name="key_w_sb")
         nc.scalar.dma_start(key_w_sb[:], key_w)
-        xn_sb = held.tile([D, T], BF16, name="xn_sb")
-        nc.scalar.dma_start(xn_sb[:], xn)
+        words = held.tile([P, S // P, D], BF16, name="words")
+        nc.sync.dma_start(words[:], table.rearrange("(h p) d -> p h d", p=P))
+        key_b_sb = held.tile([D, 1], F32, name="key_b_sb")
+        nc.scalar.dma_start(key_b_sb[:], key_b)
+        offsets = held.tile([P, N // 16], U16, name="offsets")
+        nc.sync.dma_start(offsets[:], offs)
 
         xk_ps = psum.tile([D, T], F32, name="xk_ps")
         nc.tensor.matmul(xk_ps[:], key_w_sb[:], xn_sb[:], start=True, stop=True)
@@ -54,9 +63,8 @@ def tile_end_expansionnet_v2_onnx_tensorrt_kernel(tc, table, xn, key_w, key_b, o
         p_scaled = held.tile([T, N], F32, name="p_scaled")
         nc.vector.tensor_scalar_mul(p_scaled[:], p_ps[:], INV_SQRT_D)
 
-        for s in range(stores):
-            staged = stage.tile([P, POSITIONS_PER_STORE * N], F32, name="staged")
-            for k in range(POSITIONS_PER_STORE):
-                t = s * POSITIONS_PER_STORE + k
-                nc.vector.tensor_scalar_add(staged[:, k * N : (k + 1) * N], p_scaled[:], q_scaled[:, t : t + 1])
-            nc.sync.dma_start(out[:, s * POSITIONS_PER_STORE * N : (s + 1) * POSITIONS_PER_STORE * N], staged[:])
+        scores = held.tile([P, T * N], F32, name="scores")
+        for first, count in store_pieces():
+            for t in range(first, first + count):
+                nc.vector.tensor_scalar_add(scores[:, t * N : (t + 1) * N], p_scaled[:], q_scaled[:, t : t + 1])
+            nc.sync.dma_start(out[:, first * N : (first + count) * N], scores[:, first * N : (first + count) * N])

@@ -7,7 +7,7 @@ S, D, T, N = 256, 128, 128, 128
 P = 128
 BF16, F32, U16 = mybir.dt.bfloat16, mybir.dt.float32, mybir.dt.uint16
 INV_SQRT_D = 1.0 / math.sqrt(D)
-FIRST_PIECE = 4
+FIRST_PIECE = 2
 LARGEST_PIECE = 16
 
 FLOPS = 2 * D * D * T + 2 * D * T * N + 2 * D * T * T

@@ -48,11 +48,11 @@ def tile_end_expansionnet_v2_onnx_tensorrt_kernel(tc, table, xn, key_w, key_b, o
         identity = held.tile([P, P], BF16, name="identity")
         nc.vector.memset(identity[:], 0.0)
         make_identity(nc, identity[:], nomemset=True)
-        table_t_ps = psum.tile([D, S], BF16, name="table_t_ps")
-        for h in range(S // P):
-            nc.tensor.transpose(table_t_ps[:, h * P : (h + 1) * P], words[:, h, :], identity[:])
         table_t = held.tile([D, S], BF16, name="table_t")
-        nc.vector.tensor_copy(table_t[:], table_t_ps[:])
+        for h in range(S // P):
+            block_ps = psum.tile([D, P], BF16, name=f"block_ps{h}")
+            nc.tensor.transpose(block_ps[:], words[:, h, :], identity[:])
+            nc.vector.tensor_copy(table_t[:, h * P : (h + 1) * P], block_ps[:])
 
         q_ps = psum.tile([T, T], F32, name="q_ps")
         nc.tensor.matmul(q_ps[:], xk[:], xn_sb[:], start=True, stop=True)

@@ -29,6 +29,8 @@ def tile_end_expansionnet_v2_onnx_tensorrt_kernel(tc, table, xn, key_w, key_b, o
         tc.tile_pool(name="held", bufs=1) as held,
         tc.psum_pool(name="psum", bufs=1) as psum,
     ):
+        scores = held.tile([P, T * N], F32, name="scores", align_bytes=512)
+
         xn_sb = held.tile([D, T], BF16, name="xn_sb")
         nc.sync.dma_start(xn_sb[:], xn)
         key_w_sb = held.tile([D, D], BF16, name="key_w_sb")
@@ -63,7 +65,6 @@ def tile_end_expansionnet_v2_onnx_tensorrt_kernel(tc, table, xn, key_w, key_b, o
         p_scaled = held.tile([T, N], F32, name="p_scaled")
         nc.vector.tensor_scalar_mul(p_scaled[:], p_ps[:], INV_SQRT_D)
 
-        scores = held.tile([P, T * N], F32, name="scores")
         for first, count in store_pieces():
             for t in range(first, first + count):
                 nc.vector.tensor_scalar_add(scores[:, t * N : (t + 1) * N], p_scaled[:], q_scaled[:, t : t + 1])

@@ -6,6 +6,7 @@ from concourse.masks import make_identity
 S, D, T, N = 256, 128, 128, 128
 P = 128
 BF16, F32, U16 = mybir.dt.bfloat16, mybir.dt.float32, mybir.dt.uint16
+MULT, ADD = mybir.AluOpType.mult, mybir.AluOpType.add
 INV_SQRT_D = 1.0 / math.sqrt(D)
 FIRST_PIECE = 2
 LARGEST_PIECE = 16
@@ -67,5 +68,8 @@ def tile_end_expansionnet_v2_onnx_tensorrt_kernel(tc, table, xn, key_w, key_b, o
 
         for first, count in store_pieces():
             for t in range(first, first + count):
-                nc.vector.tensor_scalar_add(scores[:, t * N : (t + 1) * N], p_scaled[:], q_scaled[:, t : t + 1])
+                if t == 0:
+                    nc.vector.tensor_scalar(scores[:, 0:N], p_ps[:], INV_SQRT_D, q_scaled[:, 0:1], MULT, ADD)
+                else:
+                    nc.vector.tensor_scalar_add(scores[:, t * N : (t + 1) * N], p_scaled[:], q_scaled[:, t : t + 1])
             nc.sync.dma_start(out[:, first * N : (first + count) * N], scores[:, first * N : (first + count) * N])

@@ -59,17 +59,13 @@ def tile_end_expansionnet_v2_onnx_tensorrt_kernel(tc, table, xn, key_w, key_b, o
 
         q_ps = psum.tile([T, T], F32, name="q_ps")
         nc.tensor.matmul(q_ps[:], xk[:], xn_sb[:], start=True, stop=True)
-        q_scaled = held.tile([T, T], F32, name="q_scaled")
-        nc.vector.tensor_scalar_mul(q_scaled[:], q_ps[:], INV_SQRT_D)
         p_ps = psum.tile([T, N], F32, name="p_ps")
         nc.tensor.matmul(p_ps[:], xk[:], table_t[:].indirect(offsets[:]), start=True, stop=True)
-        p_scaled = held.tile([T, N], F32, name="p_scaled")
-        nc.vector.tensor_scalar_mul(p_scaled[:], p_ps[:], INV_SQRT_D)
+        p_sb = held.tile([T, N], F32, name="p_sb")
+        nc.vector.tensor_copy(p_sb[:], p_ps[:])
 
         for first, count in store_pieces():
             for t in range(first, first + count):
-                if t == 0:
-                    nc.vector.tensor_scalar(scores[:, 0:N], p_ps[:], INV_SQRT_D, q_scaled[:, 0:1], MULT, ADD)
-                else:
-                    nc.vector.tensor_scalar_add(scores[:, t * N : (t + 1) * N], p_scaled[:], q_scaled[:, t : t + 1])
+                p_rows = p_ps if t == 0 else p_sb
+                nc.vector.tensor_scalar(scores[:, t * N : (t + 1) * N], p_rows[:], q_ps[:, t : t + 1], INV_SQRT_D, ADD, MULT)
             nc.sync.dma_start(out[:, first * N : (first + count) * N], scores[:, first * N : (first + count) * N])

@@ -53,11 +53,11 @@ def tile_end_expansionnet_v2_onnx_tensorrt_kernel(tc, table, xn, key_w, key_b, o
         make_identity(nc, identity[:], nomemset=True)
         table_t = held.tile([D, S], BF16, name="table_t")
         for h in range(S // P):
-            block_ps = psum.tile([D, P], BF16, name=f"block_ps{h}")
+            block_ps = psum.tile([D, P], BF16, name=f"block_ps{h}", tag=f"bank{h}")
             nc.tensor.transpose(block_ps[:], words[:, h, :], identity[:])
             nc.vector.tensor_copy(table_t[:, h * P : (h + 1) * P], block_ps[:])
 
-        q_ps = psum.tile([T, T], F32, name="q_ps")
+        q_ps = psum.tile([T, T], F32, name="q_ps", tag="bank0")
         nc.tensor.matmul(q_ps[:], xk[:], xn_sb[:], start=True, stop=True)
         p_ps = psum.tile([T, N], F32, name="p_ps")
         nc.tensor.matmul(p_ps[:], xk[:], table_t[:].indirect(offsets[:]), start=True, stop=True)

@@ -9,7 +9,6 @@ BF16, F32, U16 = mybir.dt.bfloat16, mybir.dt.float32, mybir.dt.uint16
 MULT, ADD = mybir.AluOpType.mult, mybir.AluOpType.add
 INV_SQRT_D = 1.0 / math.sqrt(D)
 FIRST_PIECE = 2
-LARGEST_PIECE = 16
 
 FLOPS = 2 * D * D * T + 2 * D * T * N + 2 * D * T * T
 
@@ -18,7 +17,7 @@ def store_pieces():
     pieces = []
     done = 0
     while done < T:
-        count = min(max(done, FIRST_PIECE), LARGEST_PIECE, T - done)
+        count = min(max(done // 2, FIRST_PIECE), T - done)
         pieces.append((done, count))
         done += count
     return pieces

@@ -8,18 +8,18 @@ P = 128
 BF16, F32, U16 = mybir.dt.bfloat16, mybir.dt.float32, mybir.dt.uint16
 MULT, ADD = mybir.AluOpType.mult, mybir.AluOpType.add
 INV_SQRT_D = 1.0 / math.sqrt(D)
-FIRST_PIECE = 2
 
 FLOPS = 2 * D * D * T + 2 * D * T * N + 2 * D * T * T
 
 
 def store_pieces():
     pieces = []
-    done = 0
+    done, count, following = 0, 1, 1
     while done < T:
-        count = min(max(done // 2, FIRST_PIECE), T - done)
+        count = min(count, T - done)
         pieces.append((done, count))
         done += count
+        count, following = following, count + following
     return pieces
 
 
@@ -36,7 +36,8 @@ def tile_end_expansionnet_v2_onnx_tensorrt_kernel(tc, table, xn, key_w, key_b, o
         key_w_sb = held.tile([D, D], BF16, name="key_w_sb")
         nc.scalar.dma_start(key_w_sb[:], key_w)
         words = held.tile([P, S // P, D], BF16, name="words")
-        nc.sync.dma_start(words[:], table.rearrange("(h p) d -> p h d", p=P))
+        for h, queue in enumerate((nc.sync, nc.scalar)):
+            queue.dma_start(words[:, h, :], table[h * P : (h + 1) * P, :])
         key_b_sb = held.tile([D, 1], F32, name="key_b_sb")
         nc.scalar.dma_start(key_b_sb[:], key_b)
         offsets = held.tile([P, N // 16], U16, name="offsets")

@@ -39,7 +39,7 @@ def tile_end_expansionnet_v2_onnx_tensorrt_kernel(tc, table, xn, key_w, key_b, o
         for h, queue in enumerate((nc.sync, nc.scalar)):
             queue.dma_start(words[:, h, :], table[h * P : (h + 1) * P, :])
         key_b_sb = held.tile([D, 1], F32, name="key_b_sb")
-        nc.scalar.dma_start(key_b_sb[:], key_b)
+        nc.sync.dma_start(key_b_sb[:], key_b)
         offsets = held.tile([P, N // 16], U16, name="offsets")
         nc.sync.dma_start(offsets[:], offs)
 

@@ -57,10 +57,10 @@ def tile_end_expansionnet_v2_onnx_tensorrt_kernel(tc, table, xn, key_w, key_b, o
             nc.tensor.transpose(block_ps[:], words[:, h, :], identity[:])
             nc.vector.tensor_copy(table_t[:, h * P : (h + 1) * P], block_ps[:])
 
-        q_ps = psum.tile([T, T], F32, name="q_ps", tag="bank0")
-        nc.tensor.matmul(q_ps[:], xk[:], xn_sb[:], start=True, stop=True)
         p_ps = psum.tile([T, N], F32, name="p_ps")
         nc.tensor.matmul(p_ps[:], xk[:], table_t[:].indirect(offsets[:]), start=True, stop=True)
+        q_ps = psum.tile([T, T], F32, name="q_ps", tag=f"bank{S // P - 1}")
+        nc.tensor.matmul(q_ps[:], xk[:], xn_sb[:], start=True, stop=True)
         p_sb = held.tile([T, N], F32, name="p_sb")
         nc.vector.tensor_copy(p_sb[:], p_ps[:])
 

import math

import concourse.mybir as mybir
from concourse.masks import make_identity

S, D, T, N = 256, 128, 128, 128
P = 128
BF16, F32, U16 = mybir.dt.bfloat16, mybir.dt.float32, mybir.dt.uint16
MULT, ADD = mybir.AluOpType.mult, mybir.AluOpType.add
INV_SQRT_D = 1.0 / math.sqrt(D)

FLOPS = 2 * D * D * T + 2 * D * T * N + 2 * D * T * T


def store_pieces():
    pieces = []
    done, count, following = 0, 1, 1
    while done < T:
        count = min(count, T - done)
        pieces.append((done, count))
        done += count
        count, following = following, count + following
    return pieces


def tile_end_expansionnet_v2_onnx_tensorrt_kernel(tc, table, xn, key_w, key_b, offs, out):
    nc = tc.nc
    with (
        tc.tile_pool(name="held", bufs=1) as held,
        tc.psum_pool(name="psum", bufs=1) as psum,
    ):
        scores = held.tile([P, T * N], F32, name="scores", align_bytes=512)

        xn_sb = held.tile([D, T], BF16, name="xn_sb")
        nc.sync.dma_start(xn_sb[:], xn)
        key_w_sb = held.tile([D, D], BF16, name="key_w_sb")
        nc.scalar.dma_start(key_w_sb[:], key_w)
        words = held.tile([P, S // P, D], BF16, name="words")
        for h, queue in enumerate((nc.sync, nc.scalar)):
            queue.dma_start(words[:, h, :], table[h * P : (h + 1) * P, :])
        key_b_sb = held.tile([D, 1], F32, name="key_b_sb")
        nc.sync.dma_start(key_b_sb[:], key_b)
        offsets = held.tile([P, N // 16], U16, name="offsets")
        nc.sync.dma_start(offsets[:], offs)

        xk_ps = psum.tile([D, T], F32, name="xk_ps")
        nc.tensor.matmul(xk_ps[:], key_w_sb[:], xn_sb[:], start=True, stop=True)
        xk = held.tile([D, T], BF16, name="xk")
        nc.vector.tensor_scalar_add(xk[:], xk_ps[:], key_b_sb[:, 0:1])

        identity = held.tile([P, P], BF16, name="identity")
        nc.vector.memset(identity[:], 0.0)
        make_identity(nc, identity[:], nomemset=True)
        table_t = held.tile([D, S], BF16, name="table_t")
        for h in range(S // P):
            block_ps = psum.tile([D, P], BF16, name=f"block_ps{h}", tag=f"bank{h}")
            nc.tensor.transpose(block_ps[:], words[:, h, :], identity[:])
            nc.vector.tensor_copy(table_t[:, h * P : (h + 1) * P], block_ps[:])

        p_ps = psum.tile([T, N], F32, name="p_ps")
        nc.tensor.matmul(p_ps[:], xk[:], table_t[:].indirect(offsets[:]), start=True, stop=True)
        q_ps = psum.tile([T, T], F32, name="q_ps", tag=f"bank{S // P - 1}")
        nc.tensor.matmul(q_ps[:], xk[:], xn_sb[:], start=True, stop=True)
        p_sb = held.tile([T, N], F32, name="p_sb")
        nc.vector.tensor_copy(p_sb[:], p_ps[:])

        for first, count in store_pieces():
            for t in range(first, first + count):
                p_rows = p_ps if t == 0 else p_sb
                nc.vector.tensor_scalar(scores[:, t * N : (t + 1) * N], p_rows[:], q_ps[:, t : t + 1], INV_SQRT_D, ADD, MULT)
            nc.sync.dma_start(out[:, first * N : (first + count) * N], scores[:, first * N : (first + count) * N])
